import numpy as np
import ml_dtypes


def mxq(x, axis, fmt="e4m3"):
    dtype, down = {"e4m3": (ml_dtypes.float8_e4m3fn, 7), "e5m2": (ml_dtypes.float8_e5m2, 14)}[fmt]
    v = np.moveaxis(np.asarray(x, np.float32).astype(ml_dtypes.bfloat16).astype(np.float64), axis, -1)
    blocks = v.reshape(v.shape[:-1] + (-1, 32))
    amax = np.abs(blocks).max(-1, keepdims=True)
    byte = np.maximum(np.where(amax > 0, np.frexp(amax)[1] - 1 + 127, 0) - down, 1)
    scale = np.exp2(byte - 127.0)
    codes = (blocks / scale).astype(np.float32).astype(dtype).astype(np.float64)
    return np.moveaxis((codes * scale).reshape(v.shape), -1, axis)


WIDE = False


def mx_kscale(k):
    if not WIDE:
        return np.ones(k)
    levels = np.array([10, -10, 5, -5, 0])
    a = np.random.permutation(np.resize(levels, k // 512 * 4)).reshape(k // 512, 4)
    idx = np.arange(k)
    return np.exp2(a[idx // 512, idx % 128 // 32])


BF16 = ml_dtypes.bfloat16


def bf(x):
    return np.asarray(x, np.float32).astype(BF16)


def f64(x):
    return np.asarray(x).astype(np.float64)


N, G, F, K, E = 512, 4096, 128, 4, 1
C = E * K * G


def setup_inputs():
    t = mx_kscale(C).reshape(E, K, G).copy()
    t[:, 0] = t[0, 0]
    t[:, K - 1] = t[:, K - 2]
    return {"x": bf(np.random.standard_normal((N, G)) * t[0, 0]),
            "z1": bf(np.random.standard_normal((E, G, N)) * t[:, 1, :, None]),
            "z2": bf(np.random.standard_normal((E, G, N)) * t[:, K - 2, :, None]),
            "S": bf(np.random.standard_normal((E, N, N)) / np.sqrt(N)),
            "weight": bf(np.random.standard_normal((F, E, K, G)) / np.sqrt(C) / t),
            "bias": bf(np.random.standard_normal((F, 1)) * 0.5)}


def reference(x, z1, z2, S, weight, bias):
    z0 = np.broadcast_to(f64(x).T[None], (E, G, N))
    z1, z2 = f64(z1), f64(z2)
    z3 = mxq(z2, 2, "e4m3") @ mxq(f64(S), 1, "e4m3")
    z = np.stack([z0, z1, z2, z3], axis=1).reshape(C, N)
    y = (mxq(f64(weight).reshape(F, C), 1, "e4m3") @ mxq(z, 0, "e4m3")) + f64(bias)
    return y[None]

@@ -1,0 +1,254 @@
+from contextlib import ExitStack
+
+import concourse.mybir as mybir
+from concourse.masks import make_identity
+
+F32 = mybir.dt.float32
+BF16 = mybir.dt.bfloat16
+U32 = mybir.dt.uint32
+U8 = mybir.dt.uint8
+FP8X4 = mybir.dt.float8_e4m3fn_x4
+
+P = 128
+NODES = 512
+FEATS = 4096
+TAPS = 4
+PASS = 512
+NG = FEATS // PASS
+
+FLOPS = 2 * FEATS * NODES * NODES + 2 * P * TAPS * FEATS * NODES
+
+
+def tile_graphfilter_pb_t_kernel(tc, x, z1, z2, S, weight, bias, out):
+    nc = tc.nc
+    with ExitStack() as ctx:
+        ctx.enter_context(tc.manual_schedule())
+        const = ctx.enter_context(tc.tile_pool(name="const", bufs=1))
+        inp = ctx.enter_context(tc.tile_pool(name="inp", bufs=NG))
+        stage = ctx.enter_context(tc.tile_pool(name="stage", bufs=2))
+        codes = ctx.enter_context(tc.tile_pool(name="codes", bufs=3))
+        ring = ctx.enter_context(tc.psum_pool(name="ring", bufs=7))
+        acc = ctx.enter_context(tc.psum_pool(name="acc", bufs=1))
+
+        ident = const.tile([P, P], F32, name="ident")
+        make_identity(nc, ident[:])
+
+        z2_in = {}
+        z1_in = {}
+        wx_in = {}
+
+        def load_z(src, store, g, tag):
+            t = inp.tile([P, 4 * NODES], BF16, name="%s_%d" % (tag, g), tag=tag)
+            nc.sync.dma_start(
+                out=t[:].rearrange("q (u r) -> q u r", u=2),
+                in_=src[0, g * PASS:(g + 1) * PASS, :].rearrange("(u q e) n -> q u (e n)", u=2, e=2),
+            )
+            store[g] = t
+
+        def load_w(i):
+            t = inp.tile([P, 4 * 1024], BF16, name="w_%d" % i, tag="wx", bufs=4)
+            nc.sync.dma_start(
+                out=t[:].rearrange("f (k c) -> f k c", k=TAPS),
+                in_=weight[:, 0, :, i * 1024:(i + 1) * 1024],
+            )
+            wx_in[i] = t
+
+        def load_x(j):
+            t = inp.tile([P, 4 * 1024], BF16, name="x_%d" % j, tag="wx", bufs=4)
+            nc.sync.dma_start(
+                out=t[:].rearrange("p (b c) -> p b c", b=4),
+                in_=x.rearrange("(b p) g -> p b g", p=P)[:, :, j * 1024:(j + 1) * 1024],
+            )
+            wx_in[4 + j] = t
+
+        def loads_for(i):
+            if i == 0:
+                load_z(z2, z2_in, 0, "z2")
+                s_t = inp.tile([P, 4 * NODES], BF16, name="s_in", tag="s_in", bufs=1)
+                nc.sync.dma_start(
+                    out=s_t[:].rearrange("q (u r) -> q u r", u=2),
+                    in_=S[0].rearrange("(u q e) m -> q u (e m)", u=2, e=2),
+                )
+                wx_in["s"] = s_t
+            load_z(z1, z1_in, i, "z1")
+            if i + 1 < NG:
+                load_z(z2, z2_in, i + 1, "z2")
+            if i < 4:
+                load_w(i)
+            else:
+                load_x(i - 4)
+
+        def transposes(words, offsets, name):
+            ps = ring.tile([P, 512], F32, name=name, tag="unit")
+            for j, o in enumerate(offsets):
+                nc.tensor.transpose(ps[:, j * P:(j + 1) * P], words[:, o:o + P], ident[:])
+            return ps
+
+        def drain_pairs(ps, dst_words):
+            nc.scalar.copy(
+                out=dst_words.rearrange("p (a c u) -> p a c u", a=2, u=2),
+                in_=ps[:].rearrange("p (a u c) -> p a c u", a=2, u=2),
+            )
+
+        def regroup(engine_copy, dst, src):
+            engine_copy(
+                out=dst[:].rearrange("p (c i t) -> p c t i", i=4, t=4),
+                in_=src[:].rearrange("p (t c i) -> p c t i", t=4, i=4),
+            )
+
+        def quantise(dst_codes, dst_scales, src):
+            nc.vector.quantize_mx(out=dst_codes.bitcast(FP8X4), scales=dst_scales, in_=src)
+
+        zt_stage = {}
+        zt_codes = {}
+
+        def tz(g):
+            st = stage.tile([P, 2048], BF16, name="ztg_%d" % g, tag="ztg", align_bytes=64)
+            words = z2_in[g][:].bitcast(F32)
+            for h in range(2):
+                ps = transposes(words, [256 * (2 * h + s) + P * u for s in range(2) for u in range(2)], "tz_%d_%d" % (g, h))
+                drain_pairs(ps, st[:].bitcast(F32)[:, 512 * h:512 * (h + 1)])
+            zt_stage[g] = st
+
+        def qzt(g):
+            c = codes.tile([P, 512], U32, name="ztc_%d" % g, tag="ztc", bufs=2, align_bytes=64)
+            s = codes.tile([P, 512], U8, name="ztp_%d" % g, tag="ztp", bufs=2, align_bytes=64)
+            quantise(c[:], s[:], zt_stage[g][:])
+            zt_codes[g] = (c, s)
+
+        wx_stage = {}
+        w_codes = {}
+        z_codes = {}
+
+        def wx(i):
+            st = stage.tile([P, 4096], BF16, name="wxg_%d" % i, tag="wxg", align_bytes=64)
+            words = wx_in[i][:].bitcast(F32)
+            for n in range(4):
+                if i < 4:
+                    offs = [512 * n + 256 * l + P * u for l in range(2) for u in range(2)]
+                else:
+                    l, h = n // 2, n % 2
+                    offs = [512 * (2 * h + b) + 256 * l + P * u for b in range(2) for u in range(2)]
+                ps = transposes(words, offs, "wx_%d_%d" % (i, n))
+                drain_pairs(ps, st[:].bitcast(F32)[:, 512 * n:512 * (n + 1)])
+            wx_stage[i] = st
+
+        def qw(i):
+            c = codes.tile([P, 1024], U32, name="wc_%d" % i, tag="wc", bufs=4, align_bytes=64)
+            s = codes.tile([P, 1024], U8, name="wp_%d" % i, tag="wp", bufs=4, align_bytes=64)
+            quantise(c[:], s[:], wx_stage[i][:])
+            w_codes[i] = (c, s)
+
+        def qx(i):
+            c = codes.tile([P, 1024], U32, name="xc_%d" % i, tag="xc", bufs=2, align_bytes=64)
+            s = codes.tile([P, 1024], U8, name="xp_%d" % i, tag="xp", bufs=2, align_bytes=64)
+            for l in range(2):
+                quantise(c[:, 512 * l:512 * (l + 1)], s[:, 512 * l:512 * (l + 1)], wx_stage[i][:, 2048 * l:2048 * (l + 1)])
+                z_codes[(0, 2 * (i - 4) + l)] = (c[:, 512 * l:512 * (l + 1)], s[:, 512 * l:512 * (l + 1)])
+
+        r_stage = {}
+
+        def rz(tap, g):
+            st = stage.tile([P, 2048], BF16, name="g%d_%d" % (tap, g), tag="g%d" % tap, align_bytes=64)
+            regroup(nc.vector.tensor_copy, st, (z1_in if tap == 1 else z2_in)[g])
+            r_stage[(tap, g)] = st
+
+        def qz(tap, g):
+            c = codes.tile([P, 512], U32, name="c%d_%d" % (tap, g), tag="c%d" % tap, align_bytes=64)
+            s = codes.tile([P, 512], U8, name="p%d_%d" % (tap, g), tag="p%d" % tap, align_bytes=64)
+            quantise(c[:], s[:], r_stage[(tap, g)][:])
+            z_codes[(tap, g)] = (c[:], s[:])
+
+        def m1(g):
+            st = stage.tile([P, 2048], BF16, name="g3_%d" % g, tag="g3", align_bytes=64)
+            zc, zs = zt_codes[g]
+            for mc in range(4):
+                ps = ring.tile([P, 512], F32, name="m1_%d_%d" % (g, mc), tag="unit")
+                for t in range(4):
+                    nc.tensor.matmul_mx(
+                        out=ps[:, P * t:P * (t + 1)],
+                        lhsT=zc[:, P * t:P * (t + 1)].bitcast(FP8X4),
+                        lhsT_scale=zs[:, P * t:P * (t + 1)],
+                        rhs=s_codes[:, P * mc:P * (mc + 1)].bitcast(FP8X4),
+                        rhs_scale=s_scales[:, P * mc:P * (mc + 1)],
+                        start=True,
+                        stop=True,
+                    )
+                nc.scalar.copy(
+                    out=st[:, 512 * mc:512 * (mc + 1)].rearrange("p (m t) -> p m t", t=4),
+                    in_=ps[:].rearrange("p (t m) -> p m t", t=4),
+                )
+            r_stage[(3, g)] = st
+
+        y_ps = acc.tile([P, NODES], F32, name="y_ps")
+        done = []
+
+        def m2(tap, g):
+            wc, ws = w_codes[g // 2]
+            o = 256 * tap + P * (g % 2)
+            zc, zs = z_codes[(tap, g)]
+            nc.tensor.matmul_mx(
+                out=y_ps[:],
+                lhsT=wc[:, o:o + P].bitcast(FP8X4),
+                lhsT_scale=ws[:, o:o + P],
+                rhs=zc.bitcast(FP8X4),
+                rhs_scale=zs,
+                start=(len(done) == 0),
+                stop=(len(done) == TAPS * NG - 1),
+            )
+            done.append((tap, g))
+
+        loads_for(0)
+        loads_for(1)
+        bias_bf = const.tile([P, 1], BF16, name="bias_bf")
+        with nc.allow_non_contiguous_dma(reason="one bias value for each partition"):
+            nc.scalar.dma_start(out=bias_bf[:], in_=bias)
+        bias_f = const.tile([P, 1], F32, name="bias_f")
+
+        tz(0)
+        s_stage = stage.tile([P, 2048], BF16, name="s_stage", tag="s_stage", bufs=1, align_bytes=64)
+        regroup(nc.scalar.copy, s_stage, wx_in["s"])
+        s_codes_t = codes.tile([P, 512], U32, name="s_codes", tag="s_codes", bufs=1, align_bytes=64)
+        s_scales_t = codes.tile([P, 512], U8, name="s_scales", tag="s_scales", bufs=1, align_bytes=64)
+        s_codes = s_codes_t[:]
+        s_scales = s_scales_t[:]
+
+        rz(2, 0)
+        qzt(0)
+        rz(1, 0)
+        qz(2, 0)
+        quantise(s_codes, s_scales, s_stage[:])
+        qz(1, 0)
+        nc.vector.tensor_copy(out=bias_f[:], in_=bias_bf[:])
+
+        for i in range(NG):
+            if i + 2 < NG:
+                loads_for(i + 2)
+            if i + 1 < NG:
+                tz(i + 1)
+            wx(i)
+            m1(i)
+            if i >= 1:
+                for tap in (1, 2, 3):
+                    m2(tap, i - 1)
+            if i >= 5:
+                m2(0, 2 * (i - 5))
+                m2(0, 2 * (i - 5) + 1)
+            if i + 1 < NG:
+                rz(2, i + 1)
+                qzt(i + 1)
+                rz(1, i + 1)
+                qz(2, i + 1)
+            if i < 4:
+                qw(i)
+            else:
+                qx(i)
+            if i + 1 < NG:
+                qz(1, i + 1)
+            qz(3, i)
+        for tap, g in ((1, 7), (2, 7), (0, 6), (0, 7), (3, 7)):
+            m2(tap, g)
+
+        y_sb = const.tile([P, NODES], F32, name="y_sb")
+        nc.vector.tensor_scalar(out=y_sb[:], in0=y_ps[:], scalar1=bias_f[:, 0:1], scalar2=None, op0=mybir.AluOpType.add)
+        nc.sync.dma_start(out=out[0], in_=y_sb[:])

@@ -15,8 +15,16 @@ FEATS = 4096
 TAPS = 4
 PASS = 512
 NG = FEATS // PASS
+HALF = NODES // 2
+ORDER = ("tz", "m1", "wx")
 
 FLOPS = 2 * FEATS * NODES * NODES + 2 * P * TAPS * FEATS * NODES
+
+
+def pass_round(tap, g):
+    if tap == 0:
+        return g // 2 + 6
+    return max(g + (0 if tap == 2 else 1), g // 2 + 2)
 
 
 def tile_graphfilter_pb_t_kernel(tc, x, z1, z2, S, weight, bias, out):
@@ -26,57 +34,47 @@ def tile_graphfilter_pb_t_kernel(tc, x, z1, z2, S, weight, bias, out):
         const = ctx.enter_context(tc.tile_pool(name="const", bufs=1))
         inp = ctx.enter_context(tc.tile_pool(name="inp", bufs=NG))
         stage = ctx.enter_context(tc.tile_pool(name="stage", bufs=2))
-        codes = ctx.enter_context(tc.tile_pool(name="codes", bufs=3))
-        ring = ctx.enter_context(tc.psum_pool(name="ring", bufs=7))
+        codes = ctx.enter_context(tc.tile_pool(name="codes", bufs=4))
+        ring = ctx.enter_context(tc.psum_pool(name="ring", bufs=6))
         acc = ctx.enter_context(tc.psum_pool(name="acc", bufs=1))
 
         ident = const.tile([P, P], F32, name="ident")
         make_identity(nc, ident[:])
 
-        z2_in = {}
-        z1_in = {}
+        z_in = {}
         wx_in = {}
 
-        def load_z(src, store, g, tag):
-            t = inp.tile([P, 4 * NODES], BF16, name="%s_%d" % (tag, g), tag=tag)
-            nc.sync.dma_start(
-                out=t[:].rearrange("q (u r) -> q u r", u=2),
-                in_=src[0, g * PASS:(g + 1) * PASS, :].rearrange("(u q e) n -> q u (e n)", u=2, e=2),
-            )
-            store[g] = t
+        def load_z(src, tap, g, pieces):
+            t = inp.tile([P, 4 * NODES], BF16, name="z%d_%d" % (tap, g), tag="z%d" % tap)
+            rows = src[0, g * PASS:(g + 1) * PASS, :]
+            if pieces == 1:
+                nc.sync.dma_start(
+                    out=t[:].rearrange("q (u r) -> q u r", u=2),
+                    in_=rows.rearrange("(u q e) n -> q u (e n)", u=2, e=2),
+                )
+            else:
+                for u in range(2):
+                    nc.sync.dma_start(
+                        out=t[:, 1024 * u:1024 * (u + 1)],
+                        in_=rows[256 * u:256 * (u + 1), :].rearrange("(q e) n -> q (e n)", e=2),
+                    )
+            z_in[(tap, g)] = t
 
-        def load_w(i):
-            t = inp.tile([P, 4 * 1024], BF16, name="w_%d" % i, tag="wx", bufs=4)
-            nc.sync.dma_start(
-                out=t[:].rearrange("f (k c) -> f k c", k=TAPS),
-                in_=weight[:, 0, :, i * 1024:(i + 1) * 1024],
-            )
+        def load_wx(i):
+            t = inp.tile([P, 4 * 1024], BF16, name="wx_%d" % i, tag="wx", bufs=4)
+            if i < 4:
+                src = weight[:, 0, :, i * 1024:(i + 1) * 1024]
+            else:
+                src = x.rearrange("(b p) g -> p b g", p=P)[:, :, (i - 4) * 1024:(i - 3) * 1024]
+            nc.sync.dma_start(out=t[:].rearrange("p (b c) -> p b c", b=4), in_=src)
             wx_in[i] = t
 
-        def load_x(j):
-            t = inp.tile([P, 4 * 1024], BF16, name="x_%d" % j, tag="wx", bufs=4)
-            nc.sync.dma_start(
-                out=t[:].rearrange("p (b c) -> p b c", b=4),
-                in_=x.rearrange("(b p) g -> p b g", p=P)[:, :, j * 1024:(j + 1) * 1024],
-            )
-            wx_in[4 + j] = t
-
-        def loads_for(i):
-            if i == 0:
-                load_z(z2, z2_in, 0, "z2")
-                s_t = inp.tile([P, 4 * NODES], BF16, name="s_in", tag="s_in", bufs=1)
-                nc.sync.dma_start(
-                    out=s_t[:].rearrange("q (u r) -> q u r", u=2),
-                    in_=S[0].rearrange("(u q e) m -> q u (e m)", u=2, e=2),
-                )
-                wx_in["s"] = s_t
-            load_z(z1, z1_in, i, "z1")
-            if i + 1 < NG:
-                load_z(z2, z2_in, i + 1, "z2")
-            if i < 4:
-                load_w(i)
-            else:
-                load_x(i - 4)
+        def loads_for(k):
+            if k < NG:
+                load_z(z1, 1, k, 1)
+                if k + 2 < NG:
+                    load_z(z2, 2, k + 2, 1)
+                load_wx(k)
 
         def transposes(words, offsets, name):
             ps = ring.tile([P, 512], F32, name=name, tag="unit")
@@ -104,7 +102,7 @@ def tile_graphfilter_pb_t_kernel(tc, x, z1, z2, S, weight, bias, out):
 
         def tz(g):
             st = stage.tile([P, 2048], BF16, name="ztg_%d" % g, tag="ztg", align_bytes=64)
-            words = z2_in[g][:].bitcast(F32)
+            words = z_in[(2, g)][:].bitcast(F32)
             for h in range(2):
                 ps = transposes(words, [256 * (2 * h + s) + P * u for s in range(2) for u in range(2)], "tz_%d_%d" % (g, h))
                 drain_pairs(ps, st[:].bitcast(F32)[:, 512 * h:512 * (h + 1)])
@@ -133,24 +131,26 @@ def tile_graphfilter_pb_t_kernel(tc, x, z1, z2, S, weight, bias, out):
                 drain_pairs(ps, st[:].bitcast(F32)[:, 512 * n:512 * (n + 1)])
             wx_stage[i] = st
 
-        def qw(i):
-            c = codes.tile([P, 1024], U32, name="wc_%d" % i, tag="wc", bufs=4, align_bytes=64)
-            s = codes.tile([P, 1024], U8, name="wp_%d" % i, tag="wp", bufs=4, align_bytes=64)
-            quantise(c[:], s[:], wx_stage[i][:])
-            w_codes[i] = (c, s)
-
-        def qx(i):
-            c = codes.tile([P, 1024], U32, name="xc_%d" % i, tag="xc", bufs=2, align_bytes=64)
-            s = codes.tile([P, 1024], U8, name="xp_%d" % i, tag="xp", bufs=2, align_bytes=64)
-            for l in range(2):
-                quantise(c[:, 512 * l:512 * (l + 1)], s[:, 512 * l:512 * (l + 1)], wx_stage[i][:, 2048 * l:2048 * (l + 1)])
-                z_codes[(0, 2 * (i - 4) + l)] = (c[:, 512 * l:512 * (l + 1)], s[:, 512 * l:512 * (l + 1)])
+        def qwx(i):
+            if i < 4:
+                c = codes.tile([P, 1024], U32, name="wc_%d" % i, tag="wc", bufs=4, align_bytes=64)
+                s = codes.tile([P, 1024], U8, name="wp_%d" % i, tag="wp", bufs=4, align_bytes=64)
+                quantise(c[:], s[:], wx_stage[i][:])
+                w_codes[i] = (c, s)
+            else:
+                c = codes.tile([P, 1024], U32, name="xc_%d" % i, tag="xc", bufs=2, align_bytes=64)
+                s = codes.tile([P, 1024], U8, name="xp_%d" % i, tag="xp", bufs=2, align_bytes=64)
+                cuts = (0, 512, 768, 1024) if i == 7 else (0, 512, 1024)
+                for a, b in zip(cuts[:-1], cuts[1:]):
+                    quantise(c[:, a:b], s[:, a:b], wx_stage[i][:, 4 * a:4 * b])
+                for l in range(2):
+                    z_codes[(0, 2 * (i - 4) + l)] = (c[:, 512 * l:512 * (l + 1)], s[:, 512 * l:512 * (l + 1)])
 
         r_stage = {}
 
         def rz(tap, g):
             st = stage.tile([P, 2048], BF16, name="g%d_%d" % (tap, g), tag="g%d" % tap, align_bytes=64)
-            regroup(nc.vector.tensor_copy, st, (z1_in if tap == 1 else z2_in)[g])
+            regroup(nc.vector.tensor_copy, st, z_in[(tap, g)])
             r_stage[(tap, g)] = st
 
         def qz(tap, g):
@@ -180,24 +180,32 @@ def tile_graphfilter_pb_t_kernel(tc, x, z1, z2, S, weight, bias, out):
                 )
             r_stage[(3, g)] = st
 
-        y_ps = acc.tile([P, NODES], F32, name="y_ps")
-        done = []
+        y_ps = [acc.tile([P, HALF], F32, name="y_ps%d" % h, tag="y%d" % h) for h in range(2)]
+        done = [[], []]
 
-        def m2(tap, g):
+        def m2(tap, g, halves):
             wc, ws = w_codes[g // 2]
             o = 256 * tap + P * (g % 2)
             zc, zs = z_codes[(tap, g)]
-            nc.tensor.matmul_mx(
-                out=y_ps[:],
-                lhsT=wc[:, o:o + P].bitcast(FP8X4),
-                lhsT_scale=ws[:, o:o + P],
-                rhs=zc.bitcast(FP8X4),
-                rhs_scale=zs,
-                start=(len(done) == 0),
-                stop=(len(done) == TAPS * NG - 1),
-            )
-            done.append((tap, g))
+            for h in halves:
+                nc.tensor.matmul_mx(
+                    out=y_ps[h][:],
+                    lhsT=wc[:, o:o + P].bitcast(FP8X4),
+                    lhsT_scale=ws[:, o:o + P],
+                    rhs=zc[:, HALF * h:HALF * (h + 1)].bitcast(FP8X4),
+                    rhs_scale=zs[:, HALF * h:HALF * (h + 1)],
+                    start=(len(done[h]) == 0),
+                    stop=(len(done[h]) == TAPS * NG - 1),
+                )
+                done[h].append((tap, g))
 
+        load_z(z2, 2, 0, 2)
+        s_in = inp.tile([P, 4 * NODES], BF16, name="s_in", tag="s_in", bufs=1)
+        nc.sync.dma_start(
+            out=s_in[:].rearrange("q (u r) -> q u r", u=2),
+            in_=S[0].rearrange("(u q e) m -> q u (e m)", u=2, e=2),
+        )
+        load_z(z2, 2, 1, 1)
         loads_for(0)
         loads_for(1)
         bias_bf = const.tile([P, 1], BF16, name="bias_bf")
@@ -207,48 +215,50 @@ def tile_graphfilter_pb_t_kernel(tc, x, z1, z2, S, weight, bias, out):
 
         tz(0)
         s_stage = stage.tile([P, 2048], BF16, name="s_stage", tag="s_stage", bufs=1, align_bytes=64)
-        regroup(nc.scalar.copy, s_stage, wx_in["s"])
+        regroup(nc.scalar.copy, s_stage, s_in)
         s_codes_t = codes.tile([P, 512], U32, name="s_codes", tag="s_codes", bufs=1, align_bytes=64)
         s_scales_t = codes.tile([P, 512], U8, name="s_scales", tag="s_scales", bufs=1, align_bytes=64)
         s_codes = s_codes_t[:]
         s_scales = s_scales_t[:]
 
         rz(2, 0)
-        qzt(0)
-        rz(1, 0)
         qz(2, 0)
+        qzt(0)
+        rz(2, 1)
         quantise(s_codes, s_scales, s_stage[:])
-        qz(1, 0)
         nc.vector.tensor_copy(out=bias_f[:], in_=bias_bf[:])
 
-        for i in range(NG):
-            if i + 2 < NG:
-                loads_for(i + 2)
+        for i in range(NG + 1):
+            loads_for(i + 2)
+            for step in ORDER:
+                if step == "tz" and i + 1 < NG:
+                    tz(i + 1)
+                if step == "m1" and i < NG:
+                    m1(i)
+                if step == "wx" and i >= 1:
+                    wx(i - 1)
+            for g in range(NG):
+                for tap in (1, 2, 3, 0):
+                    if pass_round(tap, g) == i:
+                        m2(tap, g, (0, 1))
+            if i < NG:
+                rz(1, i)
             if i + 1 < NG:
-                tz(i + 1)
-            wx(i)
-            m1(i)
-            if i >= 1:
-                for tap in (1, 2, 3):
-                    m2(tap, i - 1)
-            if i >= 5:
-                m2(0, 2 * (i - 5))
-                m2(0, 2 * (i - 5) + 1)
-            if i + 1 < NG:
-                rz(2, i + 1)
                 qzt(i + 1)
-                rz(1, i + 1)
                 qz(2, i + 1)
-            if i < 4:
-                qw(i)
-            else:
-                qx(i)
-            if i + 1 < NG:
-                qz(1, i + 1)
-            qz(3, i)
-        for tap, g in ((1, 7), (2, 7), (0, 6), (0, 7), (3, 7)):
-            m2(tap, g)
+            if i + 2 < NG:
+                rz(2, i + 2)
+            if i < NG:
+                qz(1, i)
+                qz(3, i)
+            if i >= 1:
+                qwx(i - 1)
 
+        m2(0, 6, (0, 1))
         y_sb = const.tile([P, NODES], F32, name="y_sb")
-        nc.vector.tensor_scalar(out=y_sb[:], in0=y_ps[:], scalar1=bias_f[:, 0:1], scalar2=None, op0=mybir.AluOpType.add)
-        nc.sync.dma_start(out=out[0], in_=y_sb[:])
+        for h in range(2):
+            m2(0, 7, (h,))
+        for h in range(2):
+            cols = slice(HALF * h, HALF * (h + 1))
+            nc.vector.tensor_scalar(out=y_sb[:, cols], in0=y_ps[h][:], scalar1=bias_f[:, 0:1], scalar2=None, op0=mybir.AluOpType.add)
+            nc.sync.dma_start(out=out[0][:, cols], in_=y_sb[:, cols])

@@ -211,7 +211,6 @@ def tile_graphfilter_pb_t_kernel(tc, x, z1, z2, S, weight, bias, out):
         bias_bf = const.tile([P, 1], BF16, name="bias_bf")
         with nc.allow_non_contiguous_dma(reason="one bias value for each partition"):
             nc.scalar.dma_start(out=bias_bf[:], in_=bias)
-        bias_f = const.tile([P, 1], F32, name="bias_f")
 
         tz(0)
         s_stage = stage.tile([P, 2048], BF16, name="s_stage", tag="s_stage", bufs=1, align_bytes=64)
@@ -226,7 +225,6 @@ def tile_graphfilter_pb_t_kernel(tc, x, z1, z2, S, weight, bias, out):
         qzt(0)
         rz(2, 1)
         quantise(s_codes, s_scales, s_stage[:])
-        nc.vector.tensor_copy(out=bias_f[:], in_=bias_bf[:])
 
         for i in range(NG + 1):
             loads_for(i + 2)
@@ -260,5 +258,5 @@ def tile_graphfilter_pb_t_kernel(tc, x, z1, z2, S, weight, bias, out):
             m2(0, 7, (h,))
         for h in range(2):
             cols = slice(HALF * h, HALF * (h + 1))
-            nc.vector.tensor_scalar(out=y_sb[:, cols], in0=y_ps[h][:], scalar1=bias_f[:, 0:1], scalar2=None, op0=mybir.AluOpType.add)
+            nc.vector.tensor_scalar(out=y_sb[:, cols], in0=y_ps[h][:], scalar1=bias_bf[:, 0:1], scalar2=None, op0=mybir.AluOpType.add)
             nc.sync.dma_start(out=out[0][:, cols], in_=y_sb[:, cols])

@@ -90,8 +90,8 @@ def tile_graphfilter_pb_t_kernel(tc, x, z1, z2, S, weight, bias, out):
 
         def regroup(engine_copy, dst, src):
             engine_copy(
-                out=dst[:].rearrange("p (c i t) -> p c t i", i=4, t=4),
-                in_=src[:].rearrange("p (t c i) -> p c t i", t=4, i=4),
+                out=dst[:].rearrange("p (c i t) -> p c t i", i=8, t=4),
+                in_=src[:].rearrange("p (t c i) -> p c t i", t=4, i=8),
             )
 
         def quantise(dst_codes, dst_scales, src):

@@ -16,15 +16,10 @@ TAPS = 4
 PASS = 512
 NG = FEATS // PASS
 HALF = NODES // 2
-ORDER = ("tz", "m1", "wx")
+PE_TILES = (2, 3, 4, 5, 6)
+ROUNDS = NG + 3
 
 FLOPS = 2 * FEATS * NODES * NODES + 2 * P * TAPS * FEATS * NODES
-
-
-def pass_round(tap, g):
-    if tap == 0:
-        return g // 2 + 6
-    return max(g + (0 if tap == 2 else 1), g // 2 + 2)
 
 
 def tile_graphfilter_pb_t_kernel(tc, x, z1, z2, S, weight, bias, out):
@@ -32,49 +27,44 @@ def tile_graphfilter_pb_t_kernel(tc, x, z1, z2, S, weight, bias, out):
     with ExitStack() as ctx:
         ctx.enter_context(tc.manual_schedule())
         const = ctx.enter_context(tc.tile_pool(name="const", bufs=1))
-        inp = ctx.enter_context(tc.tile_pool(name="inp", bufs=NG))
+        inp = ctx.enter_context(tc.tile_pool(name="inp", bufs=4))
         stage = ctx.enter_context(tc.tile_pool(name="stage", bufs=2))
-        codes = ctx.enter_context(tc.tile_pool(name="codes", bufs=4))
+        codes = ctx.enter_context(tc.tile_pool(name="codes", bufs=3))
         ring = ctx.enter_context(tc.psum_pool(name="ring", bufs=6))
         acc = ctx.enter_context(tc.psum_pool(name="acc", bufs=1))
 
         ident = const.tile([P, P], F32, name="ident")
         make_identity(nc, ident[:])
+        ident_bf = const.tile([P, P], BF16, name="ident_bf")
+        make_identity(nc, ident_bf[:])
 
         z_in = {}
         wx_in = {}
 
-        def load_z(src, tap, g, pieces):
+        def load_z(src, tap, g):
             t = inp.tile([P, 4 * NODES], BF16, name="z%d_%d" % (tap, g), tag="z%d" % tap)
             rows = src[0, g * PASS:(g + 1) * PASS, :]
-            if pieces == 1:
-                nc.sync.dma_start(
-                    out=t[:].rearrange("q (u r) -> q u r", u=2),
-                    in_=rows.rearrange("(u q e) n -> q u (e n)", u=2, e=2),
-                )
-            else:
+            if tap == 2 and g == 0:
                 for u in range(2):
                     nc.sync.dma_start(
                         out=t[:, 1024 * u:1024 * (u + 1)],
                         in_=rows[256 * u:256 * (u + 1), :].rearrange("(q e) n -> q (e n)", e=2),
                     )
+            else:
+                nc.sync.dma_start(
+                    out=t[:].rearrange("q (u r) -> q u r", u=2),
+                    in_=rows.rearrange("(u q e) n -> q u (e n)", u=2, e=2),
+                )
             z_in[(tap, g)] = t
 
         def load_wx(i):
-            t = inp.tile([P, 4 * 1024], BF16, name="wx_%d" % i, tag="wx", bufs=4)
+            t = inp.tile([P, 4 * 1024], BF16, name="wx_%d" % i, tag="wx")
             if i < 4:
                 src = weight[:, 0, :, i * 1024:(i + 1) * 1024]
             else:
                 src = x.rearrange("(b p) g -> p b g", p=P)[:, :, (i - 4) * 1024:(i - 3) * 1024]
             nc.sync.dma_start(out=t[:].rearrange("p (b c) -> p b c", b=4), in_=src)
             wx_in[i] = t
-
-        def loads_for(k):
-            if k < NG:
-                load_z(z1, 1, k, 1)
-                if k + 2 < NG:
-                    load_z(z2, 2, k + 2, 1)
-                load_wx(k)
 
         def transposes(words, offsets, name):
             ps = ring.tile([P, 512], F32, name=name, tag="unit")
@@ -88,10 +78,10 @@ def tile_graphfilter_pb_t_kernel(tc, x, z1, z2, S, weight, bias, out):
                 in_=ps[:].rearrange("p (a u c) -> p a c u", a=2, u=2),
             )
 
-        def regroup(engine_copy, dst, src):
-            engine_copy(
-                out=dst[:].rearrange("p (c i t) -> p c t i", i=8, t=4),
-                in_=src[:].rearrange("p (t c i) -> p c t i", t=4, i=8),
+        def regroup(dst, src, width):
+            nc.vector.tensor_copy(
+                out=dst[:].rearrange("p (c i t) -> p c t i", i=8, t=4)[:, :width // 8],
+                in_=src[:].rearrange("p (t c i) -> p c t i", t=4, i=8)[:, :width // 8],
             )
 
         def quantise(dst_codes, dst_scales, src):
@@ -109,14 +99,15 @@ def tile_graphfilter_pb_t_kernel(tc, x, z1, z2, S, weight, bias, out):
             zt_stage[g] = st
 
         def qzt(g):
-            c = codes.tile([P, 512], U32, name="ztc_%d" % g, tag="ztc", bufs=2, align_bytes=64)
-            s = codes.tile([P, 512], U8, name="ztp_%d" % g, tag="ztp", bufs=2, align_bytes=64)
+            c = codes.tile([P, 512], U32, name="ztc_%d" % g, tag="ztc", align_bytes=64)
+            s = codes.tile([P, 512], U8, name="ztp_%d" % g, tag="ztp", align_bytes=64)
             quantise(c[:], s[:], zt_stage[g][:])
             zt_codes[g] = (c, s)
 
         wx_stage = {}
         w_codes = {}
         z_codes = {}
+        fresh = []
 
         def wx(i):
             st = stage.tile([P, 4096], BF16, name="wxg_%d" % i, tag="wxg", align_bytes=64)
@@ -144,23 +135,45 @@ def tile_graphfilter_pb_t_kernel(tc, x, z1, z2, S, weight, bias, out):
                 for a, b in zip(cuts[:-1], cuts[1:]):
                     quantise(c[:, a:b], s[:, a:b], wx_stage[i][:, 4 * a:4 * b])
                 for l in range(2):
-                    z_codes[(0, 2 * (i - 4) + l)] = (c[:, 512 * l:512 * (l + 1)], s[:, 512 * l:512 * (l + 1)])
+                    g = 2 * (i - 4) + l
+                    z_codes[(0, g)] = (c[:, 512 * l:512 * (l + 1)], s[:, 512 * l:512 * (l + 1)])
+                    fresh.append((0, g))
 
         r_stage = {}
 
-        def rz(tap, g):
-            st = stage.tile([P, 2048], BF16, name="g%d_%d" % (tap, g), tag="g%d" % tap, align_bytes=64)
-            regroup(nc.vector.tensor_copy, st, z_in[(tap, g)])
-            r_stage[(tap, g)] = st
+        def new_stage(tap, g):
+            r_stage[(tap, g)] = stage.tile([P, 2048], BF16, name="g%d_%d" % (tap, g), tag="g%d" % tap, align_bytes=64)
+            return r_stage[(tap, g)]
+
+        def rz2(g):
+            regroup(new_stage(2, g), z_in[(2, g)], NODES)
+
+        def rz1_pe(g):
+            st = new_stage(1, g)
+            if g in PE_TILES:
+                ps = ring.tile([P, 1024], BF16, name="r1_%d" % g, tag="unit")
+                for u in range(2):
+                    nc.tensor.matmul(
+                        out=ps[:].rearrange("p (n u e) -> p u n e", u=2, e=2)[:, u],
+                        lhsT=ident_bf[:],
+                        rhs=z_in[(1, g)][:].rearrange("p (u e n) -> p u n e", u=2, e=2)[:, u, HALF:, :],
+                        start=True,
+                        stop=True,
+                    )
+                nc.scalar.copy(out=st[:, 1024:], in_=ps[:])
+
+        def rz1_vector(g):
+            regroup(r_stage[(1, g)], z_in[(1, g)], HALF if g in PE_TILES else NODES)
 
         def qz(tap, g):
             c = codes.tile([P, 512], U32, name="c%d_%d" % (tap, g), tag="c%d" % tap, align_bytes=64)
             s = codes.tile([P, 512], U8, name="p%d_%d" % (tap, g), tag="p%d" % tap, align_bytes=64)
             quantise(c[:], s[:], r_stage[(tap, g)][:])
             z_codes[(tap, g)] = (c[:], s[:])
+            fresh.append((tap, g))
 
         def m1(g):
-            st = stage.tile([P, 2048], BF16, name="g3_%d" % g, tag="g3", align_bytes=64)
+            st = new_stage(3, g)
             zc, zs = zt_codes[g]
             for mc in range(4):
                 ps = ring.tile([P, 512], F32, name="m1_%d_%d" % (g, mc), tag="unit")
@@ -178,7 +191,6 @@ def tile_graphfilter_pb_t_kernel(tc, x, z1, z2, S, weight, bias, out):
                     out=st[:, 512 * mc:512 * (mc + 1)].rearrange("p (m t) -> p m t", t=4),
                     in_=ps[:].rearrange("p (t m) -> p m t", t=4),
                 )
-            r_stage[(3, g)] = st
 
         y_ps = [acc.tile([P, HALF], F32, name="y_ps%d" % h, tag="y%d" % h) for h in range(2)]
         done = [[], []]
@@ -199,60 +211,62 @@ def tile_graphfilter_pb_t_kernel(tc, x, z1, z2, S, weight, bias, out):
                 )
                 done[h].append((tap, g))
 
-        load_z(z2, 2, 0, 2)
         s_in = inp.tile([P, 4 * NODES], BF16, name="s_in", tag="s_in", bufs=1)
-        nc.sync.dma_start(
-            out=s_in[:].rearrange("q (u r) -> q u r", u=2),
-            in_=S[0].rearrange("(u q e) m -> q u (e m)", u=2, e=2),
-        )
-        load_z(z2, 2, 1, 1)
-        loads_for(0)
-        loads_for(1)
-        bias_bf = const.tile([P, 1], BF16, name="bias_bf")
-        with nc.allow_non_contiguous_dma(reason="one bias value for each partition"):
-            nc.scalar.dma_start(out=bias_bf[:], in_=bias)
-
-        tz(0)
         s_stage = stage.tile([P, 2048], BF16, name="s_stage", tag="s_stage", bufs=1, align_bytes=64)
-        regroup(nc.scalar.copy, s_stage, s_in)
-        s_codes_t = codes.tile([P, 512], U32, name="s_codes", tag="s_codes", bufs=1, align_bytes=64)
-        s_scales_t = codes.tile([P, 512], U8, name="s_scales", tag="s_scales", bufs=1, align_bytes=64)
-        s_codes = s_codes_t[:]
-        s_scales = s_scales_t[:]
+        s_codes = codes.tile([P, 512], U32, name="s_codes", tag="s_codes", bufs=1, align_bytes=64)
+        s_scales = codes.tile([P, 512], U8, name="s_scales", tag="s_scales", bufs=1, align_bytes=64)
+        bias_bf = const.tile([P, 1], BF16, name="bias_bf")
 
-        rz(2, 0)
-        qz(2, 0)
-        qzt(0)
-        rz(2, 1)
-        quantise(s_codes, s_scales, s_stage[:])
+        def unit(i, lag):
+            return [i - lag] if 0 <= i - lag < NG else []
 
-        for i in range(NG + 1):
-            loads_for(i + 2)
-            for step in ORDER:
-                if step == "tz" and i + 1 < NG:
-                    tz(i + 1)
-                if step == "m1" and i < NG:
-                    m1(i)
-                if step == "wx" and i >= 1:
-                    wx(i - 1)
-            for g in range(NG):
-                for tap in (1, 2, 3, 0):
-                    if pass_round(tap, g) == i:
-                        m2(tap, g, (0, 1))
-            if i < NG:
-                rz(1, i)
-            if i + 1 < NG:
-                qzt(i + 1)
-                qz(2, i + 1)
-            if i + 2 < NG:
-                rz(2, i + 2)
-            if i < NG:
-                qz(1, i)
-                qz(3, i)
-            if i >= 1:
-                qwx(i - 1)
+        for i in range(ROUNDS):
+            for g in unit(i, 0):
+                load_z(z2, 2, g)
+            for g in unit(i, 2):
+                load_z(z1, 1, g)
+            if i == 0:
+                nc.sync.dma_start(
+                    out=s_in[:].rearrange("q (u r) -> q u r", u=2),
+                    in_=S[0].rearrange("(u q e) m -> q u (e m)", u=2, e=2),
+                )
+                with nc.allow_non_contiguous_dma(reason="one bias value for each partition"):
+                    nc.scalar.dma_start(out=bias_bf[:], in_=bias)
+            for g in unit(i, 2):
+                load_wx(g)
 
-        m2(0, 6, (0, 1))
+            ready = [(tap, g) for tap, g in fresh if g // 2 in w_codes]
+            for g in unit(i, 3):
+                wx(g)
+            if i == 1:
+                regroup(s_stage, s_in, NODES)
+            for g in unit(i, 0):
+                tz(g)
+            for g in unit(i, 2):
+                m1(g)
+                rz1_pe(g)
+            for tap, g in ready:
+                m2(tap, g, (0, 1))
+                fresh.remove((tap, g))
+
+            for g in unit(i, 1):
+                qzt(g)
+            for g in unit(i, 3):
+                rz1_vector(g)
+                qz(3, g)
+            if i == 1:
+                quantise(s_codes[:], s_scales[:], s_stage[:])
+            for g in unit(i, 3):
+                qz(1, g)
+            for g in unit(i, 1):
+                qz(2, g)
+            for g in unit(i, 3):
+                qwx(g)
+            for g in unit(i, 0):
+                rz2(g)
+
+        for tap, g in fresh[:-1]:
+            m2(tap, g, (0, 1))
         y_sb = const.tile([P, NODES], F32, name="y_sb")
         for h in range(2):
             m2(0, 7, (h,))

@@ -16,8 +16,9 @@ TAPS = 4
 PASS = 512
 NG = FEATS // PASS
 HALF = NODES // 2
-PE_TILES = (2, 3, 4, 5, 6)
-ROUNDS = NG + 3
+SHARE = 64
+SHARE_FROM = 2
+ROUNDS = NG + 4
 
 FLOPS = 2 * FEATS * NODES * NODES + 2 * P * TAPS * FEATS * NODES
 
@@ -29,14 +30,12 @@ def tile_graphfilter_pb_t_kernel(tc, x, z1, z2, S, weight, bias, out):
         const = ctx.enter_context(tc.tile_pool(name="const", bufs=1))
         inp = ctx.enter_context(tc.tile_pool(name="inp", bufs=4))
         stage = ctx.enter_context(tc.tile_pool(name="stage", bufs=2))
-        codes = ctx.enter_context(tc.tile_pool(name="codes", bufs=3))
+        codes = ctx.enter_context(tc.tile_pool(name="codes", bufs=5))
         ring = ctx.enter_context(tc.psum_pool(name="ring", bufs=6))
         acc = ctx.enter_context(tc.psum_pool(name="acc", bufs=1))
 
         ident = const.tile([P, P], F32, name="ident")
         make_identity(nc, ident[:])
-        ident_bf = const.tile([P, P], BF16, name="ident_bf")
-        make_identity(nc, ident_bf[:])
 
         z_in = {}
         wx_in = {}
@@ -78,10 +77,10 @@ def tile_graphfilter_pb_t_kernel(tc, x, z1, z2, S, weight, bias, out):
                 in_=ps[:].rearrange("p (a u c) -> p a c u", a=2, u=2),
             )
 
-        def regroup(dst, src, width):
-            nc.vector.tensor_copy(
-                out=dst[:].rearrange("p (c i t) -> p c t i", i=8, t=4)[:, :width // 8],
-                in_=src[:].rearrange("p (t c i) -> p c t i", t=4, i=8)[:, :width // 8],
+        def regroup(engine_copy, dst, src, a, b):
+            engine_copy(
+                out=dst[:].rearrange("p (c i t) -> p c t i", i=8, t=4)[:, a // 8:b // 8],
+                in_=src[:].rearrange("p (t c i) -> p c t i", t=4, i=8)[:, a // 8:b // 8],
             )
 
         def quantise(dst_codes, dst_scales, src):
@@ -99,8 +98,8 @@ def tile_graphfilter_pb_t_kernel(tc, x, z1, z2, S, weight, bias, out):
             zt_stage[g] = st
 
         def qzt(g):
-            c = codes.tile([P, 512], U32, name="ztc_%d" % g, tag="ztc", align_bytes=64)
-            s = codes.tile([P, 512], U8, name="ztp_%d" % g, tag="ztp", align_bytes=64)
+            c = codes.tile([P, 512], U32, name="ztc_%d" % g, tag="ztc", bufs=3, align_bytes=64)
+            s = codes.tile([P, 512], U8, name="ztp_%d" % g, tag="ztp", bufs=3, align_bytes=64)
             quantise(c[:], s[:], zt_stage[g][:])
             zt_codes[g] = (c, s)
 
@@ -109,18 +108,19 @@ def tile_graphfilter_pb_t_kernel(tc, x, z1, z2, S, weight, bias, out):
         z_codes = {}
         fresh = []
 
-        def wx(i):
-            st = stage.tile([P, 4096], BF16, name="wxg_%d" % i, tag="wxg", align_bytes=64)
+        def new_wx_stage(i):
+            wx_stage[i] = stage.tile([P, 4096], BF16, name="wxg_%d" % i, tag="wxg", align_bytes=64)
+
+        def wx(i, banks):
             words = wx_in[i][:].bitcast(F32)
-            for n in range(4):
+            for n in banks:
                 if i < 4:
                     offs = [512 * n + 256 * l + P * u for l in range(2) for u in range(2)]
                 else:
                     l, h = n // 2, n % 2
                     offs = [512 * (2 * h + b) + 256 * l + P * u for b in range(2) for u in range(2)]
                 ps = transposes(words, offs, "wx_%d_%d" % (i, n))
-                drain_pairs(ps, st[:].bitcast(F32)[:, 512 * n:512 * (n + 1)])
-            wx_stage[i] = st
+                drain_pairs(ps, wx_stage[i][:].bitcast(F32)[:, 512 * n:512 * (n + 1)])
 
         def qwx(i):
             if i < 4:
@@ -146,24 +146,18 @@ def tile_graphfilter_pb_t_kernel(tc, x, z1, z2, S, weight, bias, out):
             return r_stage[(tap, g)]
 
         def rz2(g):
-            regroup(new_stage(2, g), z_in[(2, g)], NODES)
+            regroup(nc.vector.tensor_copy, new_stage(2, g), z_in[(2, g)], 0, NODES)
 
-        def rz1_pe(g):
+        def share(g):
+            return SHARE if g >= SHARE_FROM else 0
+
+        def rz1_scalar(g):
             st = new_stage(1, g)
-            if g in PE_TILES:
-                ps = ring.tile([P, 1024], BF16, name="r1_%d" % g, tag="unit")
-                for u in range(2):
-                    nc.tensor.matmul(
-                        out=ps[:].rearrange("p (n u e) -> p u n e", u=2, e=2)[:, u],
-                        lhsT=ident_bf[:],
-                        rhs=z_in[(1, g)][:].rearrange("p (u e n) -> p u n e", u=2, e=2)[:, u, HALF:, :],
-                        start=True,
-                        stop=True,
-                    )
-                nc.scalar.copy(out=st[:, 1024:], in_=ps[:])
+            if share(g):
+                regroup(nc.scalar.copy, st, z_in[(1, g)], 0, share(g))
 
         def rz1_vector(g):
-            regroup(r_stage[(1, g)], z_in[(1, g)], HALF if g in PE_TILES else NODES)
+            regroup(nc.vector.tensor_copy, r_stage[(1, g)], z_in[(1, g)], share(g), NODES)
 
         def qz(tap, g):
             c = codes.tile([P, 512], U32, name="c%d_%d" % (tap, g), tag="c%d" % tap, align_bytes=64)
@@ -221,6 +215,8 @@ def tile_graphfilter_pb_t_kernel(tc, x, z1, z2, S, weight, bias, out):
             return [i - lag] if 0 <= i - lag < NG else []
 
         for i in range(ROUNDS):
+            for g in unit(i, 3):
+                load_wx(g)
             for g in unit(i, 0):
                 load_z(z2, 2, g)
             for g in unit(i, 2):
@@ -232,38 +228,44 @@ def tile_graphfilter_pb_t_kernel(tc, x, z1, z2, S, weight, bias, out):
                 )
                 with nc.allow_non_contiguous_dma(reason="one bias value for each partition"):
                     nc.scalar.dma_start(out=bias_bf[:], in_=bias)
-            for g in unit(i, 2):
-                load_wx(g)
 
             ready = [(tap, g) for tap, g in fresh if g // 2 in w_codes]
-            for g in unit(i, 3):
-                wx(g)
-            if i == 1:
-                regroup(s_stage, s_in, NODES)
-            for g in unit(i, 0):
-                tz(g)
+            half = (len(ready) + 1) // 2
             for g in unit(i, 2):
                 m1(g)
-                rz1_pe(g)
-            for tap, g in ready:
+                rz1_scalar(g)
+            for g in unit(i, 3):
+                new_wx_stage(g)
+                wx(g, (0, 1))
+            for tap, g in ready[:half]:
                 m2(tap, g, (0, 1))
-                fresh.remove((tap, g))
+            for g in unit(i, 0):
+                tz(g)
+            for g in unit(i, 3):
+                wx(g, (2, 3))
+            if i == 0:
+                regroup(nc.scalar.copy, s_stage, s_in, 0, NODES)
+            for tap, g in ready[half:]:
+                m2(tap, g, (0, 1))
+            for u in ready:
+                fresh.remove(u)
 
-            for g in unit(i, 1):
-                qzt(g)
-            for g in unit(i, 3):
-                rz1_vector(g)
-                qz(3, g)
-            if i == 1:
-                quantise(s_codes[:], s_scales[:], s_stage[:])
-            for g in unit(i, 3):
-                qz(1, g)
-            for g in unit(i, 1):
-                qz(2, g)
-            for g in unit(i, 3):
+            for g in unit(i, 4):
                 qwx(g)
             for g in unit(i, 0):
                 rz2(g)
+            for g in unit(i, 2):
+                rz1_vector(g)
+            if i == 1:
+                quantise(s_codes[:], s_scales[:], s_stage[:])
+            for g in unit(i, 0):
+                qz(2, g)
+            for g in unit(i, 2):
+                qz(3, g)
+            for g in unit(i, 0):
+                qzt(g)
+            for g in unit(i, 2):
+                qz(1, g)
 
         for tap, g in fresh[:-1]:
             m2(tap, g, (0, 1))

@@ -16,8 +16,7 @@ TAPS = 4
 PASS = 512
 NG = FEATS // PASS
 HALF = NODES // 2
-SHARE = 64
-SHARE_FROM = 2
+SHARE = 32
 ROUNDS = NG + 4
 
 FLOPS = 2 * FEATS * NODES * NODES + 2 * P * TAPS * FEATS * NODES
@@ -148,16 +147,11 @@ def tile_graphfilter_pb_t_kernel(tc, x, z1, z2, S, weight, bias, out):
         def rz2(g):
             regroup(nc.vector.tensor_copy, new_stage(2, g), z_in[(2, g)], 0, NODES)
 
-        def share(g):
-            return SHARE if g >= SHARE_FROM else 0
-
         def rz1_scalar(g):
-            st = new_stage(1, g)
-            if share(g):
-                regroup(nc.scalar.copy, st, z_in[(1, g)], 0, share(g))
+            regroup(nc.scalar.copy, new_stage(1, g), z_in[(1, g)], 0, SHARE)
 
         def rz1_vector(g):
-            regroup(nc.vector.tensor_copy, r_stage[(1, g)], z_in[(1, g)], share(g), NODES)
+            regroup(nc.vector.tensor_copy, r_stage[(1, g)], z_in[(1, g)], SHARE, NODES)
 
         def qz(tap, g):
             c = codes.tile([P, 512], U32, name="c%d_%d" % (tap, g), tag="c%d" % tap, align_bytes=64)
@@ -182,8 +176,8 @@ def tile_graphfilter_pb_t_kernel(tc, x, z1, z2, S, weight, bias, out):
                         stop=True,
                     )
                 nc.scalar.copy(
-                    out=st[:, 512 * mc:512 * (mc + 1)].rearrange("p (m t) -> p m t", t=4),
-                    in_=ps[:].rearrange("p (t m) -> p m t", t=4),
+                    out=st[:, 512 * mc:512 * (mc + 1)].rearrange("p (m i t) -> p m t i", i=2, t=4),
+                    in_=ps[:].rearrange("p (t m i) -> p m t i", t=4, i=2),
                 )
 
         y_ps = [acc.tile([P, HALF], F32, name="y_ps%d" % h, tag="y%d" % h) for h in range(2)]
@@ -215,10 +209,10 @@ def tile_graphfilter_pb_t_kernel(tc, x, z1, z2, S, weight, bias, out):
             return [i - lag] if 0 <= i - lag < NG else []
 
         for i in range(ROUNDS):
-            for g in unit(i, 3):
-                load_wx(g)
             for g in unit(i, 0):
                 load_z(z2, 2, g)
+            for g in unit(i, 3):
+                load_wx(g)
             for g in unit(i, 2):
                 load_z(z1, 1, g)
             if i == 0:
@@ -231,41 +225,40 @@ def tile_graphfilter_pb_t_kernel(tc, x, z1, z2, S, weight, bias, out):
 
             ready = [(tap, g) for tap, g in fresh if g // 2 in w_codes]
             half = (len(ready) + 1) // 2
-            for g in unit(i, 2):
-                m1(g)
-                rz1_scalar(g)
-            for g in unit(i, 3):
-                new_wx_stage(g)
-                wx(g, (0, 1))
-            for tap, g in ready[:half]:
-                m2(tap, g, (0, 1))
             for g in unit(i, 0):
                 tz(g)
+            for tap, g in ready[:half]:
+                m2(tap, g, (0, 1))
             for g in unit(i, 3):
-                wx(g, (2, 3))
+                rz1_scalar(g)
+                new_wx_stage(g)
+                wx(g, (0, 1))
             if i == 0:
                 regroup(nc.scalar.copy, s_stage, s_in, 0, NODES)
             for tap, g in ready[half:]:
                 m2(tap, g, (0, 1))
+            for g in unit(i, 3):
+                wx(g, (2, 3))
+            for g in unit(i, 2):
+                m1(g)
             for u in ready:
                 fresh.remove(u)
 
-            for g in unit(i, 4):
-                qwx(g)
+            for g in unit(i, 1):
+                qzt(g)
             for g in unit(i, 0):
                 rz2(g)
-            for g in unit(i, 2):
+            for g in unit(i, 3):
                 rz1_vector(g)
-            if i == 1:
-                quantise(s_codes[:], s_scales[:], s_stage[:])
-            for g in unit(i, 0):
-                qz(2, g)
-            for g in unit(i, 2):
+            for g in unit(i, 4):
+                qz(1, g)
+                qwx(g)
+            for g in unit(i, 3):
                 qz(3, g)
             for g in unit(i, 0):
-                qzt(g)
-            for g in unit(i, 2):
-                qz(1, g)
+                qz(2, g)
+            if i == 1:
+                quantise(s_codes[:], s_scales[:], s_stage[:])
 
         for tap, g in fresh[:-1]:
             m2(tap, g, (0, 1))

from contextlib import ExitStack

import concourse.mybir as mybir
from concourse.masks import make_identity

F32 = mybir.dt.float32
BF16 = mybir.dt.bfloat16
U32 = mybir.dt.uint32
U8 = mybir.dt.uint8
FP8X4 = mybir.dt.float8_e4m3fn_x4

P = 128
NODES = 512
FEATS = 4096
TAPS = 4
PASS = 512
NG = FEATS // PASS
HALF = NODES // 2
SHARE = 32
ROUNDS = NG + 4

FLOPS = 2 * FEATS * NODES * NODES + 2 * P * TAPS * FEATS * NODES


def tile_graphfilter_pb_t_kernel(tc, x, z1, z2, S, weight, bias, out):
    nc = tc.nc
    with ExitStack() as ctx:
        ctx.enter_context(tc.manual_schedule())
        const = ctx.enter_context(tc.tile_pool(name="const", bufs=1))
        inp = ctx.enter_context(tc.tile_pool(name="inp", bufs=4))
        stage = ctx.enter_context(tc.tile_pool(name="stage", bufs=2))
        codes = ctx.enter_context(tc.tile_pool(name="codes", bufs=5))
        ring = ctx.enter_context(tc.psum_pool(name="ring", bufs=6))
        acc = ctx.enter_context(tc.psum_pool(name="acc", bufs=1))

        ident = const.tile([P, P], F32, name="ident")
        make_identity(nc, ident[:])

        z_in = {}
        wx_in = {}

        def load_z(src, tap, g):
            t = inp.tile([P, 4 * NODES], BF16, name="z%d_%d" % (tap, g), tag="z%d" % tap)
            rows = src[0, g * PASS:(g + 1) * PASS, :]
            if tap == 2 and g == 0:
                for u in range(2):
                    nc.sync.dma_start(
                        out=t[:, 1024 * u:1024 * (u + 1)],
                        in_=rows[256 * u:256 * (u + 1), :].rearrange("(q e) n -> q (e n)", e=2),
                    )
            else:
                nc.sync.dma_start(
                    out=t[:].rearrange("q (u r) -> q u r", u=2),
                    in_=rows.rearrange("(u q e) n -> q u (e n)", u=2, e=2),
                )
            z_in[(tap, g)] = t

        def load_wx(i):
            t = inp.tile([P, 4 * 1024], BF16, name="wx_%d" % i, tag="wx")
            if i < 4:
                src = weight[:, 0, :, i * 1024:(i + 1) * 1024]
            else:
                src = x.rearrange("(b p) g -> p b g", p=P)[:, :, (i - 4) * 1024:(i - 3) * 1024]
            nc.sync.dma_start(out=t[:].rearrange("p (b c) -> p b c", b=4), in_=src)
            wx_in[i] = t

        def transposes(words, offsets, name):
            ps = ring.tile([P, 512], F32, name=name, tag="unit")
            for j, o in enumerate(offsets):
                nc.tensor.transpose(ps[:, j * P:(j + 1) * P], words[:, o:o + P], ident[:])
            return ps

        def drain_pairs(ps, dst_words):
            nc.scalar.copy(
                out=dst_words.rearrange("p (a c u) -> p a c u", a=2, u=2),
                in_=ps[:].rearrange("p (a u c) -> p a c u", a=2, u=2),
            )

        def regroup(engine_copy, dst, src, a, b):
            engine_copy(
                out=dst[:].rearrange("p (c i t) -> p c t i", i=8, t=4)[:, a // 8:b // 8],
                in_=src[:].rearrange("p (t c i) -> p c t i", t=4, i=8)[:, a // 8:b // 8],
            )

        def quantise(dst_codes, dst_scales, src):
            nc.vector.quantize_mx(out=dst_codes.bitcast(FP8X4), scales=dst_scales, in_=src)

        zt_stage = {}
        zt_codes = {}

        def tz(g):
            st = stage.tile([P, 2048], BF16, name="ztg_%d" % g, tag="ztg", align_bytes=64)
            words = z_in[(2, g)][:].bitcast(F32)
            for h in range(2):
                ps = transposes(words, [256 * (2 * h + s) + P * u for s in range(2) for u in range(2)], "tz_%d_%d" % (g, h))
                drain_pairs(ps, st[:].bitcast(F32)[:, 512 * h:512 * (h + 1)])
            zt_stage[g] = st

        def qzt(g):
            c = codes.tile([P, 512], U32, name="ztc_%d" % g, tag="ztc", bufs=3, align_bytes=64)
            s = codes.tile([P, 512], U8, name="ztp_%d" % g, tag="ztp", bufs=3, align_bytes=64)
            quantise(c[:], s[:], zt_stage[g][:])
            zt_codes[g] = (c, s)

        wx_stage = {}
        w_codes = {}
        z_codes = {}
        fresh = []

        def new_wx_stage(i):
            wx_stage[i] = stage.tile([P, 4096], BF16, name="wxg_%d" % i, tag="wxg", align_bytes=64)

        def wx(i, banks):
            words = wx_in[i][:].bitcast(F32)
            for n in banks:
                if i < 4:
                    offs = [512 * n + 256 * l + P * u for l in range(2) for u in range(2)]
                else:
                    l, h = n // 2, n % 2
                    offs = [512 * (2 * h + b) + 256 * l + P * u for b in range(2) for u in range(2)]
                ps = transposes(words, offs, "wx_%d_%d" % (i, n))
                drain_pairs(ps, wx_stage[i][:].bitcast(F32)[:, 512 * n:512 * (n + 1)])

        def qwx(i):
            if i < 4:
                c = codes.tile([P, 1024], U32, name="wc_%d" % i, tag="wc", bufs=4, align_bytes=64)
                s = codes.tile([P, 1024], U8, name="wp_%d" % i, tag="wp", bufs=4, align_bytes=64)
                quantise(c[:], s[:], wx_stage[i][:])
                w_codes[i] = (c, s)
            else:
                c = codes.tile([P, 1024], U32, name="xc_%d" % i, tag="xc", bufs=2, align_bytes=64)
                s = codes.tile([P, 1024], U8, name="xp_%d" % i, tag="xp", bufs=2, align_bytes=64)
                cuts = (0, 512, 768, 1024) if i == 7 else (0, 512, 1024)
                for a, b in zip(cuts[:-1], cuts[1:]):
                    quantise(c[:, a:b], s[:, a:b], wx_stage[i][:, 4 * a:4 * b])
                for l in range(2):
                    g = 2 * (i - 4) + l
                    z_codes[(0, g)] = (c[:, 512 * l:512 * (l + 1)], s[:, 512 * l:512 * (l + 1)])
                    fresh.append((0, g))

        r_stage = {}

        def new_stage(tap, g):
            r_stage[(tap, g)] = stage.tile([P, 2048], BF16, name="g%d_%d" % (tap, g), tag="g%d" % tap, align_bytes=64)
            return r_stage[(tap, g)]

        def rz2(g):
            regroup(nc.vector.tensor_copy, new_stage(2, g), z_in[(2, g)], 0, NODES)

        def rz1_scalar(g):
            regroup(nc.scalar.copy, new_stage(1, g), z_in[(1, g)], 0, SHARE)

        def rz1_vector(g):
            regroup(nc.vector.tensor_copy, r_stage[(1, g)], z_in[(1, g)], SHARE, NODES)

        def qz(tap, g):
            c = codes.tile([P, 512], U32, name="c%d_%d" % (tap, g), tag="c%d" % tap, align_bytes=64)
            s = codes.tile([P, 512], U8, name="p%d_%d" % (tap, g), tag="p%d" % tap, align_bytes=64)
            quantise(c[:], s[:], r_stage[(tap, g)][:])
            z_codes[(tap, g)] = (c[:], s[:])
            fresh.append((tap, g))

        def m1(g):
            st = new_stage(3, g)
            zc, zs = zt_codes[g]
            for mc in range(4):
                ps = ring.tile([P, 512], F32, name="m1_%d_%d" % (g, mc), tag="unit")
                for t in range(4):
                    nc.tensor.matmul_mx(
                        out=ps[:, P * t:P * (t + 1)],
                        lhsT=zc[:, P * t:P * (t + 1)].bitcast(FP8X4),
                        lhsT_scale=zs[:, P * t:P * (t + 1)],
                        rhs=s_codes[:, P * mc:P * (mc + 1)].bitcast(FP8X4),
                        rhs_scale=s_scales[:, P * mc:P * (mc + 1)],
                        start=True,
                        stop=True,
                    )
                nc.scalar.copy(
                    out=st[:, 512 * mc:512 * (mc + 1)].rearrange("p (m i t) -> p m t i", i=2, t=4),
                    in_=ps[:].rearrange("p (t m i) -> p m t i", t=4, i=2),
                )

        y_ps = [acc.tile([P, HALF], F32, name="y_ps%d" % h, tag="y%d" % h) for h in range(2)]
        done = [[], []]

        def m2(tap, g, halves):
            wc, ws = w_codes[g // 2]
            o = 256 * tap + P * (g % 2)
            zc, zs = z_codes[(tap, g)]
            for h in halves:
                nc.tensor.matmul_mx(
                    out=y_ps[h][:],
                    lhsT=wc[:, o:o + P].bitcast(FP8X4),
                    lhsT_scale=ws[:, o:o + P],
                    rhs=zc[:, HALF * h:HALF * (h + 1)].bitcast(FP8X4),
                    rhs_scale=zs[:, HALF * h:HALF * (h + 1)],
                    start=(len(done[h]) == 0),
                    stop=(len(done[h]) == TAPS * NG - 1),
                )
                done[h].append((tap, g))

        s_in = inp.tile([P, 4 * NODES], BF16, name="s_in", tag="s_in", bufs=1)
        s_stage = stage.tile([P, 2048], BF16, name="s_stage", tag="s_stage", bufs=1, align_bytes=64)
        s_codes = codes.tile([P, 512], U32, name="s_codes", tag="s_codes", bufs=1, align_bytes=64)
        s_scales = codes.tile([P, 512], U8, name="s_scales", tag="s_scales", bufs=1, align_bytes=64)
        bias_bf = const.tile([P, 1], BF16, name="bias_bf")

        def unit(i, lag):
            return [i - lag] if 0 <= i - lag < NG else []

        for i in range(ROUNDS):
            for g in unit(i, 0):
                load_z(z2, 2, g)
            for g in unit(i, 3):
                load_wx(g)
            for g in unit(i, 2):
                load_z(z1, 1, g)
            if i == 0:
                nc.sync.dma_start(
                    out=s_in[:].rearrange("q (u r) -> q u r", u=2),
                    in_=S[0].rearrange("(u q e) m -> q u (e m)", u=2, e=2),
                )
                with nc.allow_non_contiguous_dma(reason="one bias value for each partition"):
                    nc.scalar.dma_start(out=bias_bf[:], in_=bias)

            ready = [(tap, g) for tap, g in fresh if g // 2 in w_codes]
            half = (len(ready) + 1) // 2
            for g in unit(i, 0):
                tz(g)
            for tap, g in ready[:half]:
                m2(tap, g, (0, 1))
            for g in unit(i, 3):
                rz1_scalar(g)
                new_wx_stage(g)
                wx(g, (0, 1))
            if i == 0:
                regroup(nc.scalar.copy, s_stage, s_in, 0, NODES)
            for tap, g in ready[half:]:
                m2(tap, g, (0, 1))
            for g in unit(i, 3):
                wx(g, (2, 3))
            for g in unit(i, 2):
                m1(g)
            for u in ready:
                fresh.remove(u)

            for g in unit(i, 1):
                qzt(g)
            for g in unit(i, 0):
                rz2(g)
            for g in unit(i, 3):
                rz1_vector(g)
            for g in unit(i, 4):
                qz(1, g)
                qwx(g)
            for g in unit(i, 3):
                qz(3, g)
            for g in unit(i, 0):
                qz(2, g)
            if i == 1:
                quantise(s_codes[:], s_scales[:], s_stage[:])

        for tap, g in fresh[:-1]:
            m2(tap, g, (0, 1))
        y_sb = const.tile([P, NODES], F32, name="y_sb")
        for h in range(2):
            m2(0, 7, (h,))
        for h in range(2):
            cols = slice(HALF * h, HALF * (h + 1))
            nc.vector.tensor_scalar(out=y_sb[:, cols], in0=y_ps[h][:], scalar1=bias_bf[:, 0:1], scalar2=None, op0=mybir.AluOpType.add)
            nc.sync.dma_start(out=out[0][:, cols], in_=y_sb[:, cols])
